import numpy as np
import ml_dtypes


def mxq(x, axis, fmt="e4m3"):
    dtype, down = {"e4m3": (ml_dtypes.float8_e4m3fn, 7), "e5m2": (ml_dtypes.float8_e5m2, 14)}[fmt]
    v = np.moveaxis(np.asarray(x, np.float32).astype(ml_dtypes.bfloat16).astype(np.float64), axis, -1)
    blocks = v.reshape(v.shape[:-1] + (-1, 32))
    amax = np.abs(blocks).max(-1, keepdims=True)
    byte = np.maximum(np.where(amax > 0, np.frexp(amax)[1] - 1 + 127, 0) - down, 1)
    scale = np.exp2(byte - 127.0)
    codes = (blocks / scale).astype(np.float32).astype(dtype).astype(np.float64)
    return np.moveaxis((codes * scale).reshape(v.shape), -1, axis)


WIDE = False


def mx_kscale(k):
    if not WIDE:
        return np.ones(k)
    levels = np.array([30, -30])
    if k % 512:
        return np.exp2(np.random.permutation(np.resize(levels, k // 32))).repeat(32)
    a = np.empty((k // 512, 16))
    for p in range(k // 512):
        a[p, :8] = np.random.permutation(np.resize(levels, 8))
        for g in range(8):
            far = levels[np.abs(levels - a[p, g]) >= 10]
            a[p, g + 8] = far[np.random.randint(len(far))]
    return np.exp2(a.ravel()).repeat(32)


BF16 = ml_dtypes.bfloat16


def bf(x):
    return np.asarray(x, np.float32).astype(BF16)


def f64(x):
    return np.asarray(x).astype(np.float64)


N, E, C, D1, D2 = 1024, 2048, 512, 2, 2
T2 = D2 + 1


def shift_down(y, k):
    return np.pad(y, ((k, 0), (0, 0)))[:y.shape[0]] if k > 0 else y


def log_softmax(z):
    d = z - z.max(-1, keepdims=True)
    return d - np.log(np.exp(d).sum(-1, keepdims=True))


def setup_inputs():
    s = mx_kscale(C)
    return {"H": bf(np.tanh(np.random.standard_normal((N, C))) * s),
            "W2": bf(np.random.standard_normal((T2, C, C)) * 2.0 / np.sqrt(C) / s[None, :, None]),
            "b2": bf(np.random.standard_normal((1, C)) * 0.2)}


def reference(H, W2, b2):
    G = mxq(f64(H), 1, "e5m2") @ mxq(f64(W2), 1, "e5m2")
    Z = sum(shift_down(G[j], D2 - j) for j in range(T2)) + T2 * f64(b2)[0]
    return log_softmax(Z)

@@ -1,0 +1,282 @@
+from contextlib import ExitStack
+
+import concourse.mybir as mybir
+from concourse.masks import make_identity
+
+F32 = mybir.dt.float32
+BF16 = mybir.dt.bfloat16
+I32 = mybir.dt.int32
+U32 = mybir.dt.uint32
+U8 = mybir.dt.uint8
+FP8X4 = mybir.dt.float8_e5m2_x4
+ALU = mybir.AluOpType
+ACT = mybir.ActivationFunctionType
+AXIS = mybir.AxisListType
+
+ROWS, C, TAPS = 1024, 512, 3
+P = 128
+PACK = 4
+SLOTS = ROWS // P
+PAIRS = SLOTS // 2
+FLOPS = 2 * TAPS * ROWS * C * C
+
+VECTOR_CLASSES = 304
+ORDER = [2, 3, 4, 5, 6, 7, 0, 1]
+SCALAR_FINALS = 4
+
+EDGES = 24
+HALF_STEP = 0.125
+DEGREE = 8
+COUNT, OFFSET, NEG_MAX, STEPS = DEGREE - 1, DEGREE, DEGREE + 1, DEGREE + 2
+
+
+def tile_predictor_pb_kernel(tc, H, W2, b2, out):
+    nc = tc.nc
+    h_rows = H.rearrange("(m s) k -> m s k", s=SLOTS)
+    out_rows = out.rearrange("(m s) n -> m s n", s=SLOTS)
+
+    with ExitStack() as ctx:
+        sb = ctx.enter_context(tc.tile_pool(name="sb", bufs=1))
+        ps = ctx.enter_context(tc.psum_pool(name="ps", bufs=1))
+        ctx.enter_context(tc.manual_schedule())
+
+        w_raw = [sb.tile([P, PACK, C], BF16, name="w_raw%d" % j, align_bytes=64) for j in range(TAPS)]
+        w_grouped = [sb.tile([P, C, PACK], BF16, name="w_grouped%d" % j, align_bytes=64) for j in range(TAPS)]
+        w_codes = [sb.tile([P, C], U32, name="w_codes%d" % j, align_bytes=64) for j in range(TAPS)]
+        w_scales = [sb.tile([P, C], U8, name="w_scales%d" % j, align_bytes=64) for j in range(TAPS)]
+        h_raw = [sb.tile([P, 2, C], BF16, name="h_raw%d" % g, align_bytes=64) for g in range(PAIRS)]
+        h_grouped = [sb.tile([P, 2, P, PACK], BF16, name="h_grouped%d" % g, align_bytes=64) for g in range(PAIRS)]
+        h_codes = [sb.tile([P, 2, P], U32, name="h_codes%d" % g, align_bytes=64) for g in range(PAIRS + 1)]
+        h_scales = [sb.tile([P, 2, P], U8, name="h_scales%d" % g, align_bytes=64) for g in range(PAIRS + 1)]
+        identity = sb.tile([P, P], F32, name="identity")
+        bias_row = sb.tile([P, C], BF16, name="bias_row")
+        threes = sb.tile([P, P], BF16, name="threes")
+        bias = sb.tile([P, C], F32, name="bias")
+        factors = sb.tile([P, SLOTS, 16], F32, name="factors")
+        terms = sb.tile([P, SLOTS, 16], F32, name="terms")
+        sums = sb.tile([P, SLOTS], F32, name="sums")
+        inverse = sb.tile([P, SLOTS], F32, name="inverse")
+        shift = sb.tile([P, SLOTS, 16], F32, name="shift")
+        steps = sb.tile([P, EDGES], F32, name="steps")
+        edges = sb.tile([P, EDGES], F32, name="edges")
+        signs = sb.tile([P, SLOTS, EDGES], F32, name="signs")
+        divisors = sb.tile([P, SLOTS, DEGREE - 1], F32, name="divisors")
+        z = [sb.tile([P, C], F32, name="z%d" % s) for s in range(SLOTS)]
+        result = [sb.tile([P, C], F32, name="result%d" % s) for s in range(SLOTS)]
+        exps = [sb.tile([P, C], BF16, name="exps%d" % s) for s in range(2)]
+        acc = {}
+        turned = {}
+
+        def load_w(j):
+            nc.sync.dma_start(out=w_raw[j][:], in_=W2[j].rearrange("(p t) n -> p t n", t=PACK))
+
+        def load_h(g):
+            nc.sync.dma_start(out=h_raw[g][:], in_=h_rows[:, 2 * g : 2 * g + 2, :])
+
+        def group_w(engine_copy, j, lo, hi):
+            engine_copy(
+                out=w_grouped[j][:, lo:hi, :].rearrange("p (c i) t -> p c t i", i=4),
+                in_=w_raw[j][:, :, lo:hi].rearrange("p t (c i) -> p c t i", i=4),
+            )
+
+        def group_w_vector(j):
+            group_w(nc.vector.tensor_copy, j, 0, VECTOR_CLASSES)
+
+        def group_w_scalar(j):
+            group_w(nc.scalar.copy, j, VECTOR_CLASSES, C)
+
+        def quantize_w(j):
+            nc.vector.quantize_mx(
+                out=w_codes[j][:].bitcast(FP8X4),
+                scales=w_scales[j][:],
+                in_=w_grouped[j][:].rearrange("p n t -> p (n t)"),
+            )
+
+        def transpose_h(g):
+            bank = ps.tile([P, 2, 2, P], F32, name="turned%d" % g, tag="turned", bufs=2)
+            turned[g] = bank
+            for a in range(2):
+                words = h_raw[g][:, a, :].bitcast(F32)
+                for u in range(2):
+                    nc.tensor.transpose(bank[:, a, u, :], words[:, u : 2 * P : 2], identity[:])
+
+        def group_h(g):
+            words = h_grouped[g][:].rearrange("p a m t -> p (a m t)").bitcast(F32)
+            nc.scalar.copy(
+                out=words.rearrange("p (a m u) -> p a m u", a=2, u=2),
+                in_=turned[g][:].rearrange("p a u m -> p a m u"),
+            )
+
+        def quantize_h(g):
+            nc.vector.quantize_mx(
+                out=h_codes[g][:].rearrange("p a m -> p (a m)").bitcast(FP8X4),
+                scales=h_scales[g][:].rearrange("p a m -> p (a m)"),
+                in_=h_grouped[g][:].rearrange("p a m t -> p (a m t)"),
+            )
+
+        def shift_last_pair():
+            nc.gpsimd.tensor_copy(
+                out=h_codes[PAIRS][:, :, 1:P].bitcast(I32), in_=h_codes[PAIRS - 1][:, :, 0 : P - 1].bitcast(I32)
+            )
+            nc.gpsimd.tensor_copy(out=h_scales[PAIRS][:, :, 1:P], in_=h_scales[PAIRS - 1][:, :, 0 : P - 1])
+
+        def multiply(s, j):
+            source = s - (TAPS - 1) + j
+            g, a = divmod(source, 2)
+            if source < 0:
+                g = PAIRS
+            if j == 0:
+                acc[s] = ps.tile([P, C], F32, name="acc%d" % s, tag="acc", bufs=5)
+            nc.tensor.matmul_mx(
+                out=acc[s][:],
+                lhsT=h_codes[g][:, a, :].bitcast(FP8X4),
+                lhsT_scale=h_scales[g][:, a, :],
+                rhs=w_codes[j][:].bitcast(FP8X4),
+                rhs_scale=w_scales[j][:],
+                start=(j == 0),
+                stop=(j == TAPS - 1),
+            )
+
+        def add_bias(s):
+            nc.vector.tensor_tensor(out=z[s][:], in0=acc[s][:], in1=bias[:], op=ALU.add)
+
+        def row_max(s):
+            nc.vector.tensor_reduce(out=terms[:, s, NEG_MAX : NEG_MAX + 1], in_=z[s][:], axis=AXIS.X, op=ALU.max, negate=True)
+
+        def exp_sum(s):
+            nc.scalar.activation(
+                out=exps[s % 2][:], in_=z[s][:], func=ACT.Exp, bias=terms[:, s, NEG_MAX : NEG_MAX + 1], accum_out=sums[:, s : s + 1]
+            )
+
+        def log_seed(s):
+            nc.scalar.activation(
+                out=signs[:, s, :],
+                in_=edges[:],
+                func=ACT.Sign,
+                scale=-1.0,
+                bias=sums[:, s : s + 1],
+                accum_out=terms[:, s, COUNT : COUNT + 1],
+            )
+
+        def log_inverse(s):
+            nc.scalar.activation(out=inverse[:, s : s + 1], in_=terms[:, s, COUNT : COUNT + 1], func=ACT.Exp,
+                                 scale=-HALF_STEP, bias=-HALF_STEP * (EDGES + 1))
+
+        def log_rest(s):
+            nc.scalar.activation(
+                out=factors[:, s, 0:DEGREE],
+                in_=inverse[:, s : s + 1].to_broadcast([P, DEGREE]),
+                func=ACT.Identity,
+                scale=sums[:, s : s + 1],
+                bias=-1.0,
+            )
+
+        def log_series(s):
+            nc.vector.tensor_tensor_scan(
+                out=shift[:, s, 0:STEPS],
+                data0=factors[:, s, 0:STEPS],
+                data1=terms[:, s, 0:STEPS],
+                initial=(-1.0) ** (DEGREE + 1) / (DEGREE * HALF_STEP),
+                op0=ALU.mult,
+                op1=ALU.add,
+            )
+
+        def finish_scalar(s):
+            nc.scalar.activation(out=result[s][:], in_=z[s][:], func=ACT.Identity, bias=shift[:, s, NEG_MAX : NEG_MAX + 1])
+            nc.sync.dma_start(out=out_rows[:, s, :], in_=result[s][:])
+
+        def finish_vector(s):
+            nc.vector.tensor_scalar(
+                out=result[s][:], in0=z[s][:], scalar1=shift[:, s, NEG_MAX : NEG_MAX + 1], scalar2=None, op0=ALU.add
+            )
+            nc.sync.dma_start(out=out_rows[:, s, :], in_=result[s][:])
+
+        nc.vector.memset(bias_row[:], 0.0)
+        load_w(0)
+        nc.sync.dma_start(out=bias_row[0:1, :], in_=b2)
+        load_h(0)
+        load_w(1)
+        load_h(1)
+        load_w(2)
+        load_h(2)
+        load_h(3)
+        nc.gpsimd.iota(steps[:], pattern=[[1, EDGES]], base=1, channel_multiplier=0, allow_small_or_imprecise_dtypes=True)
+        nc.scalar.activation(out=edges[:], in_=steps[:], func=ACT.Exp, scale=2.0 * HALF_STEP)
+        make_identity(nc, identity[:])
+        nc.gpsimd.memset(h_scales[PAIRS - 1][:], 127)
+        nc.gpsimd.memset(h_scales[PAIRS][:], 127)
+        nc.gpsimd.memset(h_codes[PAIRS][:].bitcast(I32), 0)
+        nc.vector.memset(threes[:], float(TAPS))
+        nc.vector.memset(factors[:, :, OFFSET : OFFSET + 1], 1.0)
+        nc.vector.memset(factors[:, :, NEG_MAX : NEG_MAX + 1], -HALF_STEP)
+        nc.vector.memset(terms[:, :, OFFSET : OFFSET + 1], float(EDGES + 1))
+        for c in range(DEGREE - 1):
+            power = DEGREE - 1 - c
+            nc.vector.memset(divisors[:, :, c : c + 1], (-1.0) ** (power + 1) * power * HALF_STEP)
+        nc.vector.reciprocal(out=terms[:, :, 0 : DEGREE - 1], in_=divisors[:])
+
+        group_w_vector(0)
+        group_w_scalar(0)
+        transpose_h(0)
+        quantize_w(0)
+        group_h(0)
+        group_w_vector(1)
+        group_w_scalar(1)
+        quantize_h(0)
+        multiply(2, 0)
+        multiply(3, 0)
+        bias_bank = ps.tile([P, C], F32, name="bias_bank")
+        nc.tensor.matmul(out=bias_bank[:], lhsT=threes[:], rhs=bias_row[:], start=True, stop=True)
+        transpose_h(1)
+        quantize_w(1)
+        group_h(1)
+        multiply(2, 1)
+        group_w_vector(2)
+        group_w_scalar(2)
+        quantize_h(1)
+        multiply(3, 1)
+        multiply(4, 0)
+        multiply(5, 0)
+        multiply(4, 1)
+        transpose_h(2)
+        nc.scalar.copy(out=bias[:], in_=bias_bank[:])
+        quantize_w(2)
+        group_h(2)
+        multiply(2, 2)
+        multiply(3, 2)
+        transpose_h(3)
+        quantize_h(2)
+        group_h(3)
+        add_bias(2)
+        multiply(4, 2)
+        multiply(5, 1)
+        multiply(5, 2)
+        multiply(6, 0)
+        multiply(6, 1)
+        add_bias(3)
+        quantize_h(3)
+        shift_last_pair()
+
+        n = len(ORDER)
+        for i in range(n + 3):
+            if i < n:
+                row_max(ORDER[i])
+                exp_sum(ORDER[i])
+            if 4 <= i + 4 < n:
+                for j in range(TAPS):
+                    if not (ORDER[i + 4] == 6 and j < 2):
+                        multiply(ORDER[i + 4], j)
+            if i + 2 < n:
+                add_bias(ORDER[i + 2])
+            if 0 <= i - 1 < n:
+                log_inverse(ORDER[i - 1])
+            if 0 <= i - 2 < n:
+                log_series(ORDER[i - 2])
+            if 0 <= i - 3 < SCALAR_FINALS:
+                finish_scalar(ORDER[i - 3])
+            if i < n:
+                log_seed(ORDER[i])
+            if 0 <= i - 1 < n:
+                log_rest(ORDER[i - 1])
+            if SCALAR_FINALS <= i - 2 < n:
+                finish_vector(ORDER[i - 2])

@@ -1,3 +1,4 @@
+import math
 from contextlib import ExitStack
 
 import concourse.mybir as mybir
@@ -20,14 +21,15 @@ SLOTS = ROWS // P
 PAIRS = SLOTS // 2
 FLOPS = 2 * TAPS * ROWS * C * C
 
-VECTOR_CLASSES = 304
+VECTOR_CLASSES = [336, 368, 320]
+VECTOR_FINALS = 4
 ORDER = [2, 3, 4, 5, 6, 7, 0, 1]
-SCALAR_FINALS = 4
 
-EDGES = 24
-HALF_STEP = 0.125
-DEGREE = 8
-COUNT, OFFSET, NEG_MAX, STEPS = DEGREE - 1, DEGREE, DEGREE + 1, DEGREE + 2
+STEP = 0.4375
+NODES = 68
+UNITS = 8
+EULER_GAMMA = 0.5772156649015329
+TOP = (UNITS - 0.5) * STEP - EULER_GAMMA - math.log(4.0 / math.pi)
 
 
 def tile_predictor_pb_kernel(tc, H, W2, b2, out):
@@ -52,15 +54,13 @@ def tile_predictor_pb_kernel(tc, H, W2, b2, out):
         bias_row = sb.tile([P, C], BF16, name="bias_row")
         threes = sb.tile([P, P], BF16, name="threes")
         bias = sb.tile([P, C], F32, name="bias")
-        factors = sb.tile([P, SLOTS, 16], F32, name="factors")
-        terms = sb.tile([P, SLOTS, 16], F32, name="terms")
+        counts = sb.tile([P, NODES], F32, name="counts")
+        nodes = sb.tile([P, NODES + UNITS], F32, name="nodes")
+        neg_max = sb.tile([P, SLOTS], F32, name="neg_max")
         sums = sb.tile([P, SLOTS], F32, name="sums")
-        inverse = sb.tile([P, SLOTS], F32, name="inverse")
-        shift = sb.tile([P, SLOTS, 16], F32, name="shift")
-        steps = sb.tile([P, EDGES], F32, name="steps")
-        edges = sb.tile([P, EDGES], F32, name="edges")
-        signs = sb.tile([P, SLOTS, EDGES], F32, name="signs")
-        divisors = sb.tile([P, SLOTS, DEGREE - 1], F32, name="divisors")
+        logs = sb.tile([P, SLOTS], F32, name="logs")
+        shift = sb.tile([P, SLOTS, 8], F32, name="shift")
+        tanhs = [sb.tile([P, NODES + UNITS], F32, name="tanhs%d" % s) for s in range(2)]
         z = [sb.tile([P, C], F32, name="z%d" % s) for s in range(SLOTS)]
         result = [sb.tile([P, C], F32, name="result%d" % s) for s in range(SLOTS)]
         exps = [sb.tile([P, C], BF16, name="exps%d" % s) for s in range(2)]
@@ -80,10 +80,10 @@ def tile_predictor_pb_kernel(tc, H, W2, b2, out):
             )
 
         def group_w_vector(j):
-            group_w(nc.vector.tensor_copy, j, 0, VECTOR_CLASSES)
+            group_w(nc.vector.tensor_copy, j, 0, VECTOR_CLASSES[j])
 
         def group_w_scalar(j):
-            group_w(nc.scalar.copy, j, VECTOR_CLASSES, C)
+            group_w(nc.scalar.copy, j, VECTOR_CLASSES[j], C)
 
         def quantize_w(j):
             nc.vector.quantize_mx(
@@ -141,55 +141,45 @@ def tile_predictor_pb_kernel(tc, H, W2, b2, out):
             nc.vector.tensor_tensor(out=z[s][:], in0=acc[s][:], in1=bias[:], op=ALU.add)
 
         def row_max(s):
-            nc.vector.tensor_reduce(out=terms[:, s, NEG_MAX : NEG_MAX + 1], in_=z[s][:], axis=AXIS.X, op=ALU.max, negate=True)
+            nc.vector.tensor_reduce(out=neg_max[:, s : s + 1], in_=z[s][:], axis=AXIS.X, op=ALU.max, negate=True)
 
         def exp_sum(s):
             nc.scalar.activation(
-                out=exps[s % 2][:], in_=z[s][:], func=ACT.Exp, bias=terms[:, s, NEG_MAX : NEG_MAX + 1], accum_out=sums[:, s : s + 1]
+                out=exps[s % 2][:], in_=z[s][:], func=ACT.Exp, bias=neg_max[:, s : s + 1], accum_out=sums[:, s : s + 1]
             )
 
-        def log_seed(s):
+        def log_sum(s):
             nc.scalar.activation(
-                out=signs[:, s, :],
-                in_=edges[:],
-                func=ACT.Sign,
-                scale=-1.0,
-                bias=sums[:, s : s + 1],
-                accum_out=terms[:, s, COUNT : COUNT + 1],
+                out=tanhs[s % 2][:], in_=nodes[:], func=ACT.Tanh, scale=sums[:, s : s + 1], accum_out=logs[:, s : s + 1]
             )
 
-        def log_inverse(s):
-            nc.scalar.activation(out=inverse[:, s : s + 1], in_=terms[:, s, COUNT : COUNT + 1], func=ACT.Exp,
-                                 scale=-HALF_STEP, bias=-HALF_STEP * (EDGES + 1))
-
-        def log_rest(s):
+        def row_shift(s):
             nc.scalar.activation(
-                out=factors[:, s, 0:DEGREE],
-                in_=inverse[:, s : s + 1].to_broadcast([P, DEGREE]),
-                func=ACT.Identity,
-                scale=sums[:, s : s + 1],
-                bias=-1.0,
+                out=shift[:, s, 0:1], in_=logs[:, s : s + 1], func=ACT.Identity, scale=-STEP, bias=neg_max[:, s : s + 1]
             )
 
-        def log_series(s):
-            nc.vector.tensor_tensor_scan(
-                out=shift[:, s, 0:STEPS],
-                data0=factors[:, s, 0:STEPS],
-                data1=terms[:, s, 0:STEPS],
-                initial=(-1.0) ** (DEGREE + 1) / (DEGREE * HALF_STEP),
-                op0=ALU.mult,
-                op1=ALU.add,
+        def finish(engine, s):
+            engine.tensor_scalar(
+                out=result[s][:], in0=z[s][:], scalar1=shift[:, s, 0:1], scalar2=1.0, op0=ALU.add, op1=ALU.mult
             )
-
-        def finish_scalar(s):
-            nc.scalar.activation(out=result[s][:], in_=z[s][:], func=ACT.Identity, bias=shift[:, s, NEG_MAX : NEG_MAX + 1])
             nc.sync.dma_start(out=out_rows[:, s, :], in_=result[s][:])
 
         def finish_vector(s):
-            nc.vector.tensor_scalar(
-                out=result[s][:], in0=z[s][:], scalar1=shift[:, s, NEG_MAX : NEG_MAX + 1], scalar2=None, op0=ALU.add
+            finish(nc.vector, s)
+
+        def finish_gpsimd(s):
+            nc.gpsimd.tensor_scalar(
+                out=shift[:, s, 0:1], in0=logs[:, s : s + 1], scalar1=-STEP, scalar2=neg_max[:, s : s + 1],
+                op0=ALU.mult, op1=ALU.add,
             )
-            nc.sync.dma_start(out=out_rows[:, s, :], in_=result[s][:])
+            finish(nc.gpsimd, s)
+
+        def spread_bias():
+            turned["bias"] = ps.tile([P, C], F32, name="bias_bank")
+            nc.tensor.matmul(out=turned["bias"][:], lhsT=threes[:], rhs=bias_row[:], start=True, stop=True)
+
+        def copy_bias():
+            nc.scalar.copy(out=bias[:], in_=turned["bias"][:])
 
         nc.vector.memset(bias_row[:], 0.0)
         load_w(0)
@@ -200,83 +190,55 @@ def tile_predictor_pb_kernel(tc, H, W2, b2, out):
         load_w(2)
         load_h(2)
         load_h(3)
-        nc.gpsimd.iota(steps[:], pattern=[[1, EDGES]], base=1, channel_multiplier=0, allow_small_or_imprecise_dtypes=True)
-        nc.scalar.activation(out=edges[:], in_=steps[:], func=ACT.Exp, scale=2.0 * HALF_STEP)
+        nc.gpsimd.iota(counts[:], pattern=[[1, NODES]], base=1 - NODES, channel_multiplier=0, allow_small_or_imprecise_dtypes=True)
+        nc.scalar.activation(out=nodes[:, 0:NODES], in_=counts[:], func=ACT.Exp, scale=STEP, bias=TOP)
         make_identity(nc, identity[:])
         nc.gpsimd.memset(h_scales[PAIRS - 1][:], 127)
         nc.gpsimd.memset(h_scales[PAIRS][:], 127)
         nc.gpsimd.memset(h_codes[PAIRS][:].bitcast(I32), 0)
         nc.vector.memset(threes[:], float(TAPS))
-        nc.vector.memset(factors[:, :, OFFSET : OFFSET + 1], 1.0)
-        nc.vector.memset(factors[:, :, NEG_MAX : NEG_MAX + 1], -HALF_STEP)
-        nc.vector.memset(terms[:, :, OFFSET : OFFSET + 1], float(EDGES + 1))
-        for c in range(DEGREE - 1):
-            power = DEGREE - 1 - c
-            nc.vector.memset(divisors[:, :, c : c + 1], (-1.0) ** (power + 1) * power * HALF_STEP)
-        nc.vector.reciprocal(out=terms[:, :, 0 : DEGREE - 1], in_=divisors[:])
+        nc.vector.memset(nodes[:, NODES:], -64.0)
 
+        spread_bias()
+        transpose_h(0)
         group_w_vector(0)
         group_w_scalar(0)
-        transpose_h(0)
+        copy_bias()
         quantize_w(0)
-        group_h(0)
+        transpose_h(1)
         group_w_vector(1)
         group_w_scalar(1)
-        quantize_h(0)
-        multiply(2, 0)
-        multiply(3, 0)
-        bias_bank = ps.tile([P, C], F32, name="bias_bank")
-        nc.tensor.matmul(out=bias_bank[:], lhsT=threes[:], rhs=bias_row[:], start=True, stop=True)
-        transpose_h(1)
-        quantize_w(1)
+        group_h(0)
         group_h(1)
-        multiply(2, 1)
+        quantize_w(1)
+        quantize_h(0)
+        transpose_h(2)
+        transpose_h(3)
         group_w_vector(2)
         group_w_scalar(2)
         quantize_h(1)
-        multiply(3, 1)
-        multiply(4, 0)
-        multiply(5, 0)
-        multiply(4, 1)
-        transpose_h(2)
-        nc.scalar.copy(out=bias[:], in_=bias_bank[:])
-        quantize_w(2)
         group_h(2)
-        multiply(2, 2)
-        multiply(3, 2)
-        transpose_h(3)
-        quantize_h(2)
         group_h(3)
-        add_bias(2)
-        multiply(4, 2)
-        multiply(5, 1)
-        multiply(5, 2)
-        multiply(6, 0)
-        multiply(6, 1)
-        add_bias(3)
-        quantize_h(3)
-        shift_last_pair()
+        quantize_w(2)
+        quantize_h(2)
 
         n = len(ORDER)
-        for i in range(n + 3):
-            if i < n:
+        for i in range(-2, n + 2):
+            if i + 2 < n:
+                for j in range(TAPS):
+                    multiply(ORDER[i + 2], j)
+            if 0 <= i + 1 < n:
+                add_bias(ORDER[i + 1])
+            if i == -1:
+                quantize_h(3)
+                shift_last_pair()
+            if 0 <= i < n:
                 row_max(ORDER[i])
                 exp_sum(ORDER[i])
-            if 4 <= i + 4 < n:
-                for j in range(TAPS):
-                    if not (ORDER[i + 4] == 6 and j < 2):
-                        multiply(ORDER[i + 4], j)
-            if i + 2 < n:
-                add_bias(ORDER[i + 2])
             if 0 <= i - 1 < n:
-                log_inverse(ORDER[i - 1])
-            if 0 <= i - 2 < n:
-                log_series(ORDER[i - 2])
-            if 0 <= i - 3 < SCALAR_FINALS:
-                finish_scalar(ORDER[i - 3])
-            if i < n:
-                log_seed(ORDER[i])
-            if 0 <= i - 1 < n:
-                log_rest(ORDER[i - 1])
-            if SCALAR_FINALS <= i - 2 < n:
+                log_sum(ORDER[i - 1])
+            if 0 <= i - 1 < n - VECTOR_FINALS:
+                finish_gpsimd(ORDER[i - 1])
+            if n - VECTOR_FINALS <= i - 2:
+                row_shift(ORDER[i - 2])
                 finish_vector(ORDER[i - 2])

@@ -21,8 +21,9 @@ SLOTS = ROWS // P
 PAIRS = SLOTS // 2
 FLOPS = 2 * TAPS * ROWS * C * C
 
-VECTOR_CLASSES = [336, 368, 320]
-VECTOR_FINALS = 4
+VECTOR_CLASSES = [352, 384, 352]
+VECTOR_FINALS = 3
+BIAS_PASSES = 1
 ORDER = [2, 3, 4, 5, 6, 7, 0, 1]
 
 STEP = 0.4375
@@ -52,7 +53,7 @@ def tile_predictor_pb_kernel(tc, H, W2, b2, out):
         h_scales = [sb.tile([P, 2, P], U8, name="h_scales%d" % g, align_bytes=64) for g in range(PAIRS + 1)]
         identity = sb.tile([P, P], F32, name="identity")
         bias_row = sb.tile([P, C], BF16, name="bias_row")
-        threes = sb.tile([P, P], BF16, name="threes")
+        ones = sb.tile([P, P], BF16, name="ones")
         bias = sb.tile([P, C], F32, name="bias")
         counts = sb.tile([P, NODES], F32, name="counts")
         nodes = sb.tile([P, NODES + UNITS], F32, name="nodes")
@@ -63,6 +64,7 @@ def tile_predictor_pb_kernel(tc, H, W2, b2, out):
         tanhs = [sb.tile([P, NODES + UNITS], F32, name="tanhs%d" % s) for s in range(2)]
         z = [sb.tile([P, C], F32, name="z%d" % s) for s in range(SLOTS)]
         result = [sb.tile([P, C], F32, name="result%d" % s) for s in range(SLOTS)]
+        centred = {s: sb.tile([P, C], F32, name="centred%d" % s) for s in ORDER[SLOTS - VECTOR_FINALS :]}
         exps = [sb.tile([P, C], BF16, name="exps%d" % s) for s in range(2)]
         acc = {}
         turned = {}
@@ -115,9 +117,7 @@ def tile_predictor_pb_kernel(tc, H, W2, b2, out):
             )
 
         def shift_last_pair():
-            nc.gpsimd.tensor_copy(
-                out=h_codes[PAIRS][:, :, 1:P].bitcast(I32), in_=h_codes[PAIRS - 1][:, :, 0 : P - 1].bitcast(I32)
-            )
+            nc.scalar.copy(out=h_codes[PAIRS][:, :, 1:P], in_=h_codes[PAIRS - 1][:, :, 0 : P - 1])
             nc.gpsimd.tensor_copy(out=h_scales[PAIRS][:, :, 1:P], in_=h_scales[PAIRS - 1][:, :, 0 : P - 1])
 
         def multiply(s, j):
@@ -138,7 +138,7 @@ def tile_predictor_pb_kernel(tc, H, W2, b2, out):
             )
 
         def add_bias(s):
-            nc.vector.tensor_tensor(out=z[s][:], in0=acc[s][:], in1=bias[:], op=ALU.add)
+            nc.vector.tensor_tensor(out=z[s][:], in0=bias[:], in1=acc[s][:], op=ALU.add)
 
         def row_max(s):
             nc.vector.tensor_reduce(out=neg_max[:, s : s + 1], in_=z[s][:], axis=AXIS.X, op=ALU.max, negate=True)
@@ -153,30 +153,34 @@ def tile_predictor_pb_kernel(tc, H, W2, b2, out):
                 out=tanhs[s % 2][:], in_=nodes[:], func=ACT.Tanh, scale=sums[:, s : s + 1], accum_out=logs[:, s : s + 1]
             )
 
+        def centre(s):
+            nc.vector.tensor_scalar(
+                out=centred[s][:], in0=z[s][:], scalar1=neg_max[:, s : s + 1], scalar2=1.0 / STEP, op0=ALU.add, op1=ALU.mult
+            )
+
+        def finish_centred(s):
+            nc.vector.tensor_scalar(
+                out=result[s][:], in0=centred[s][:], scalar1=logs[:, s : s + 1], scalar2=STEP, op0=ALU.subtract, op1=ALU.mult
+            )
+            nc.sync.dma_start(out=out_rows[:, s, :], in_=result[s][:])
+
         def row_shift(s):
             nc.scalar.activation(
                 out=shift[:, s, 0:1], in_=logs[:, s : s + 1], func=ACT.Identity, scale=-STEP, bias=neg_max[:, s : s + 1]
             )
 
-        def finish(engine, s):
-            engine.tensor_scalar(
+        def finish_gpsimd(s):
+            nc.gpsimd.tensor_scalar(
                 out=result[s][:], in0=z[s][:], scalar1=shift[:, s, 0:1], scalar2=1.0, op0=ALU.add, op1=ALU.mult
             )
             nc.sync.dma_start(out=out_rows[:, s, :], in_=result[s][:])
 
-        def finish_vector(s):
-            finish(nc.vector, s)
-
-        def finish_gpsimd(s):
-            nc.gpsimd.tensor_scalar(
-                out=shift[:, s, 0:1], in0=logs[:, s : s + 1], scalar1=-STEP, scalar2=neg_max[:, s : s + 1],
-                op0=ALU.mult, op1=ALU.add,
-            )
-            finish(nc.gpsimd, s)
-
         def spread_bias():
             turned["bias"] = ps.tile([P, C], F32, name="bias_bank")
-            nc.tensor.matmul(out=turned["bias"][:], lhsT=threes[:], rhs=bias_row[:], start=True, stop=True)
+            for j in range(BIAS_PASSES):
+                nc.tensor.matmul(
+                    out=turned["bias"][:], lhsT=ones[:], rhs=bias_row[:], start=(j == 0), stop=(j == BIAS_PASSES - 1)
+                )
 
         def copy_bias():
             nc.scalar.copy(out=bias[:], in_=turned["bias"][:])
@@ -196,49 +200,61 @@ def tile_predictor_pb_kernel(tc, H, W2, b2, out):
         nc.gpsimd.memset(h_scales[PAIRS - 1][:], 127)
         nc.gpsimd.memset(h_scales[PAIRS][:], 127)
         nc.gpsimd.memset(h_codes[PAIRS][:].bitcast(I32), 0)
-        nc.vector.memset(threes[:], float(TAPS))
+        nc.vector.memset(ones[:], float(TAPS // BIAS_PASSES))
         nc.vector.memset(nodes[:, NODES:], -64.0)
 
-        spread_bias()
+        early = [(2, 0), (3, 0), (2, 1)]
         transpose_h(0)
+        spread_bias()
         group_w_vector(0)
         group_w_scalar(0)
-        copy_bias()
         quantize_w(0)
+        group_h(0)
         transpose_h(1)
         group_w_vector(1)
         group_w_scalar(1)
-        group_h(0)
-        group_h(1)
-        quantize_w(1)
         quantize_h(0)
+        multiply(2, 0)
+        multiply(3, 0)
+        quantize_w(1)
         transpose_h(2)
-        transpose_h(3)
+        multiply(2, 1)
         group_w_vector(2)
         group_w_scalar(2)
+        group_h(1)
+        copy_bias()
         quantize_h(1)
-        group_h(2)
-        group_h(3)
         quantize_w(2)
+        group_h(2)
         quantize_h(2)
 
         n = len(ORDER)
-        for i in range(-2, n + 2):
+        for i in range(-2, n):
             if i + 2 < n:
                 for j in range(TAPS):
-                    multiply(ORDER[i + 2], j)
+                    if (ORDER[i + 2], j) not in early:
+                        multiply(ORDER[i + 2], j)
+            if i == -1:
+                transpose_h(3)
+                group_h(3)
             if 0 <= i + 1 < n:
                 add_bias(ORDER[i + 1])
-            if i == -1:
-                quantize_h(3)
-                shift_last_pair()
-            if 0 <= i < n:
+            if i >= 0:
                 row_max(ORDER[i])
                 exp_sum(ORDER[i])
-            if 0 <= i - 1 < n:
-                log_sum(ORDER[i - 1])
+            if i == 0:
+                quantize_h(3)
+                shift_last_pair()
             if 0 <= i - 1 < n - VECTOR_FINALS:
+                row_shift(ORDER[i - 1])
                 finish_gpsimd(ORDER[i - 1])
-            if n - VECTOR_FINALS <= i - 2:
-                row_shift(ORDER[i - 2])
-                finish_vector(ORDER[i - 2])
+            if 0 <= i < n - 2:
+                log_sum(ORDER[i])
+        for s in ORDER[n - 2 :]:
+            log_sum(s)
+        tail = ORDER[n - VECTOR_FINALS :]
+        centre(tail[0])
+        for i in range(VECTOR_FINALS):
+            if i + 1 < VECTOR_FINALS:
+                centre(tail[i + 1])
+            finish_centred(tail[i])

import math
from contextlib import ExitStack

import concourse.mybir as mybir
from concourse.masks import make_identity

F32 = mybir.dt.float32
BF16 = mybir.dt.bfloat16
I32 = mybir.dt.int32
U32 = mybir.dt.uint32
U8 = mybir.dt.uint8
FP8X4 = mybir.dt.float8_e5m2_x4
ALU = mybir.AluOpType
ACT = mybir.ActivationFunctionType
AXIS = mybir.AxisListType

ROWS, C, TAPS = 1024, 512, 3
P = 128
PACK = 4
SLOTS = ROWS // P
PAIRS = SLOTS // 2
FLOPS = 2 * TAPS * ROWS * C * C

VECTOR_CLASSES = [352, 384, 352]
VECTOR_FINALS = 3
BIAS_PASSES = 1
ORDER = [2, 3, 4, 5, 6, 7, 0, 1]

STEP = 0.4375
NODES = 68
UNITS = 8
EULER_GAMMA = 0.5772156649015329
TOP = (UNITS - 0.5) * STEP - EULER_GAMMA - math.log(4.0 / math.pi)


def tile_predictor_pb_kernel(tc, H, W2, b2, out):
    nc = tc.nc
    h_rows = H.rearrange("(m s) k -> m s k", s=SLOTS)
    out_rows = out.rearrange("(m s) n -> m s n", s=SLOTS)

    with ExitStack() as ctx:
        sb = ctx.enter_context(tc.tile_pool(name="sb", bufs=1))
        ps = ctx.enter_context(tc.psum_pool(name="ps", bufs=1))
        ctx.enter_context(tc.manual_schedule())

        w_raw = [sb.tile([P, PACK, C], BF16, name="w_raw%d" % j, align_bytes=64) for j in range(TAPS)]
        w_grouped = [sb.tile([P, C, PACK], BF16, name="w_grouped%d" % j, align_bytes=64) for j in range(TAPS)]
        w_codes = [sb.tile([P, C], U32, name="w_codes%d" % j, align_bytes=64) for j in range(TAPS)]
        w_scales = [sb.tile([P, C], U8, name="w_scales%d" % j, align_bytes=64) for j in range(TAPS)]
        h_raw = [sb.tile([P, 2, C], BF16, name="h_raw%d" % g, align_bytes=64) for g in range(PAIRS)]
        h_grouped = [sb.tile([P, 2, P, PACK], BF16, name="h_grouped%d" % g, align_bytes=64) for g in range(PAIRS)]
        h_codes = [sb.tile([P, 2, P], U32, name="h_codes%d" % g, align_bytes=64) for g in range(PAIRS + 1)]
        h_scales = [sb.tile([P, 2, P], U8, name="h_scales%d" % g, align_bytes=64) for g in range(PAIRS + 1)]
        identity = sb.tile([P, P], F32, name="identity")
        bias_row = sb.tile([P, C], BF16, name="bias_row")
        ones = sb.tile([P, P], BF16, name="ones")
        bias = sb.tile([P, C], F32, name="bias")
        counts = sb.tile([P, NODES], F32, name="counts")
        nodes = sb.tile([P, NODES + UNITS], F32, name="nodes")
        neg_max = sb.tile([P, SLOTS], F32, name="neg_max")
        sums = sb.tile([P, SLOTS], F32, name="sums")
        logs = sb.tile([P, SLOTS], F32, name="logs")
        shift = sb.tile([P, SLOTS, 8], F32, name="shift")
        tanhs = [sb.tile([P, NODES + UNITS], F32, name="tanhs%d" % s) for s in range(2)]
        z = [sb.tile([P, C], F32, name="z%d" % s) for s in range(SLOTS)]
        result = [sb.tile([P, C], F32, name="result%d" % s) for s in range(SLOTS)]
        centred = {s: sb.tile([P, C], F32, name="centred%d" % s) for s in ORDER[SLOTS - VECTOR_FINALS :]}
        exps = [sb.tile([P, C], BF16, name="exps%d" % s) for s in range(2)]
        acc = {}
        turned = {}

        def load_w(j):
            nc.sync.dma_start(out=w_raw[j][:], in_=W2[j].rearrange("(p t) n -> p t n", t=PACK))

        def load_h(g):
            nc.sync.dma_start(out=h_raw[g][:], in_=h_rows[:, 2 * g : 2 * g + 2, :])

        def group_w(engine_copy, j, lo, hi):
            engine_copy(
                out=w_grouped[j][:, lo:hi, :].rearrange("p (c i) t -> p c t i", i=4),
                in_=w_raw[j][:, :, lo:hi].rearrange("p t (c i) -> p c t i", i=4),
            )

        def group_w_vector(j):
            group_w(nc.vector.tensor_copy, j, 0, VECTOR_CLASSES[j])

        def group_w_scalar(j):
            group_w(nc.scalar.copy, j, VECTOR_CLASSES[j], C)

        def quantize_w(j):
            nc.vector.quantize_mx(
                out=w_codes[j][:].bitcast(FP8X4),
                scales=w_scales[j][:],
                in_=w_grouped[j][:].rearrange("p n t -> p (n t)"),
            )

        def transpose_h(g):
            bank = ps.tile([P, 2, 2, P], F32, name="turned%d" % g, tag="turned", bufs=2)
            turned[g] = bank
            for a in range(2):
                words = h_raw[g][:, a, :].bitcast(F32)
                for u in range(2):
                    nc.tensor.transpose(bank[:, a, u, :], words[:, u : 2 * P : 2], identity[:])

        def group_h(g):
            words = h_grouped[g][:].rearrange("p a m t -> p (a m t)").bitcast(F32)
            nc.scalar.copy(
                out=words.rearrange("p (a m u) -> p a m u", a=2, u=2),
                in_=turned[g][:].rearrange("p a u m -> p a m u"),
            )

        def quantize_h(g):
            nc.vector.quantize_mx(
                out=h_codes[g][:].rearrange("p a m -> p (a m)").bitcast(FP8X4),
                scales=h_scales[g][:].rearrange("p a m -> p (a m)"),
                in_=h_grouped[g][:].rearrange("p a m t -> p (a m t)"),
            )

        def shift_last_pair():
            nc.scalar.copy(out=h_codes[PAIRS][:, :, 1:P], in_=h_codes[PAIRS - 1][:, :, 0 : P - 1])
            nc.gpsimd.tensor_copy(out=h_scales[PAIRS][:, :, 1:P], in_=h_scales[PAIRS - 1][:, :, 0 : P - 1])

        def multiply(s, j):
            source = s - (TAPS - 1) + j
            g, a = divmod(source, 2)
            if source < 0:
                g = PAIRS
            if j == 0:
                acc[s] = ps.tile([P, C], F32, name="acc%d" % s, tag="acc", bufs=5)
            nc.tensor.matmul_mx(
                out=acc[s][:],
                lhsT=h_codes[g][:, a, :].bitcast(FP8X4),
                lhsT_scale=h_scales[g][:, a, :],
                rhs=w_codes[j][:].bitcast(FP8X4),
                rhs_scale=w_scales[j][:],
                start=(j == 0),
                stop=(j == TAPS - 1),
            )

        def add_bias(s):
            nc.vector.tensor_tensor(out=z[s][:], in0=bias[:], in1=acc[s][:], op=ALU.add)

        def row_max(s):
            nc.vector.tensor_reduce(out=neg_max[:, s : s + 1], in_=z[s][:], axis=AXIS.X, op=ALU.max, negate=True)

        def exp_sum(s):
            nc.scalar.activation(
                out=exps[s % 2][:], in_=z[s][:], func=ACT.Exp, bias=neg_max[:, s : s + 1], accum_out=sums[:, s : s + 1]
            )

        def log_sum(s):
            nc.scalar.activation(
                out=tanhs[s % 2][:], in_=nodes[:], func=ACT.Tanh, scale=sums[:, s : s + 1], accum_out=logs[:, s : s + 1]
            )

        def centre(s):
            nc.vector.tensor_scalar(
                out=centred[s][:], in0=z[s][:], scalar1=neg_max[:, s : s + 1], scalar2=1.0 / STEP, op0=ALU.add, op1=ALU.mult
            )

        def finish_centred(s):
            nc.vector.tensor_scalar(
                out=result[s][:], in0=centred[s][:], scalar1=logs[:, s : s + 1], scalar2=STEP, op0=ALU.subtract, op1=ALU.mult
            )
            nc.sync.dma_start(out=out_rows[:, s, :], in_=result[s][:])

        def row_shift(s):
            nc.scalar.activation(
                out=shift[:, s, 0:1], in_=logs[:, s : s + 1], func=ACT.Identity, scale=-STEP, bias=neg_max[:, s : s + 1]
            )

        def finish_gpsimd(s):
            nc.gpsimd.tensor_scalar(
                out=result[s][:], in0=z[s][:], scalar1=shift[:, s, 0:1], scalar2=1.0, op0=ALU.add, op1=ALU.mult
            )
            nc.sync.dma_start(out=out_rows[:, s, :], in_=result[s][:])

        def spread_bias():
            turned["bias"] = ps.tile([P, C], F32, name="bias_bank")
            for j in range(BIAS_PASSES):
                nc.tensor.matmul(
                    out=turned["bias"][:], lhsT=ones[:], rhs=bias_row[:], start=(j == 0), stop=(j == BIAS_PASSES - 1)
                )

        def copy_bias():
            nc.scalar.copy(out=bias[:], in_=turned["bias"][:])

        nc.vector.memset(bias_row[:], 0.0)
        load_w(0)
        nc.sync.dma_start(out=bias_row[0:1, :], in_=b2)
        load_h(0)
        load_w(1)
        load_h(1)
        load_w(2)
        load_h(2)
        load_h(3)
        nc.gpsimd.iota(counts[:], pattern=[[1, NODES]], base=1 - NODES, channel_multiplier=0, allow_small_or_imprecise_dtypes=True)
        nc.scalar.activation(out=nodes[:, 0:NODES], in_=counts[:], func=ACT.Exp, scale=STEP, bias=TOP)
        make_identity(nc, identity[:])
        nc.gpsimd.memset(h_scales[PAIRS - 1][:], 127)
        nc.gpsimd.memset(h_scales[PAIRS][:], 127)
        nc.gpsimd.memset(h_codes[PAIRS][:].bitcast(I32), 0)
        nc.vector.memset(ones[:], float(TAPS // BIAS_PASSES))
        nc.vector.memset(nodes[:, NODES:], -64.0)

        early = [(2, 0), (3, 0), (2, 1)]
        transpose_h(0)
        spread_bias()
        group_w_vector(0)
        group_w_scalar(0)
        quantize_w(0)
        group_h(0)
        transpose_h(1)
        group_w_vector(1)
        group_w_scalar(1)
        quantize_h(0)
        multiply(2, 0)
        multiply(3, 0)
        quantize_w(1)
        transpose_h(2)
        multiply(2, 1)
        group_w_vector(2)
        group_w_scalar(2)
        group_h(1)
        copy_bias()
        quantize_h(1)
        quantize_w(2)
        group_h(2)
        quantize_h(2)

        n = len(ORDER)
        for i in range(-2, n):
            if i + 2 < n:
                for j in range(TAPS):
                    if (ORDER[i + 2], j) not in early:
                        multiply(ORDER[i + 2], j)
            if i == -1:
                transpose_h(3)
                group_h(3)
            if 0 <= i + 1 < n:
                add_bias(ORDER[i + 1])
            if i >= 0:
                row_max(ORDER[i])
                exp_sum(ORDER[i])
            if i == 0:
                quantize_h(3)
                shift_last_pair()
            if 0 <= i - 1 < n - VECTOR_FINALS:
                row_shift(ORDER[i - 1])
                finish_gpsimd(ORDER[i - 1])
            if 0 <= i < n - 2:
                log_sum(ORDER[i])
        for s in ORDER[n - 2 :]:
            log_sum(s)
        tail = ORDER[n - VECTOR_FINALS :]
        centre(tail[0])
        for i in range(VECTOR_FINALS):
            if i + 1 < VECTOR_FINALS:
                centre(tail[i + 1])
            finish_centred(tail[i])
